import numpy as np
import ml_dtypes


def mxq(x, axis, fmt="e4m3"):
    dtype, down = {"e4m3": (ml_dtypes.float8_e4m3fn, 7), "e5m2": (ml_dtypes.float8_e5m2, 14)}[fmt]
    v = np.moveaxis(np.asarray(x, np.float32).astype(ml_dtypes.bfloat16).astype(np.float64), axis, -1)
    blocks = v.reshape(v.shape[:-1] + (-1, 32))
    amax = np.abs(blocks).max(-1, keepdims=True)
    byte = np.maximum(np.where(amax > 0, np.frexp(amax)[1] - 1 + 127, 0) - down, 1)
    scale = np.exp2(byte - 127.0)
    codes = (blocks / scale).astype(np.float32).astype(dtype).astype(np.float64)
    return np.moveaxis((codes * scale).reshape(v.shape), -1, axis)


WIDE = False


def mx_kscale(k):
    if not WIDE:
        return np.ones(k)
    levels = np.array([10, -10, 5, -5, 0])
    a = np.random.permutation(np.resize(levels, k // 512 * 4)).reshape(k // 512, 4)
    idx = np.arange(k)
    return np.exp2(a[idx // 512, idx % 128 // 32])


BF16 = ml_dtypes.bfloat16


def bf(x):
    return np.asarray(x, np.float32).astype(BF16)


def f64(x):
    return np.asarray(x).astype(np.float64)


B, S, P, H, DH, DM = 16, 256, 256, 4, 128, 1024
D = H * DH
MASKED = -1.0e30


def with_mean(n, a, b):
    return np.random.standard_normal((B, H, n, DH)) * a + np.random.standard_normal((B, H, DH))[:, :, None, :] * b


def setup_inputs():
    t = mx_kscale(D)
    th = t.reshape(H, DH)[:, None, :]
    return {"q": bf(np.random.standard_normal((B, H, S, DH))),
            "k_cache": bf(with_mean(P, 0.4, 0.5)),
            "v_cache": bf(with_mean(P, 1.0, 1.0) * th),
            "k_new": bf(with_mean(S, 0.4, 0.5)),
            "v_new": bf(with_mean(S, 1.0, 1.0) * th),
            "wo": bf(np.random.standard_normal((DM, D)) * 2.0 / np.sqrt(D) / t[None, :])}


def reference(q, k_cache, v_cache, k_new, v_new, wo):
    qf = f64(q)
    s_cache = qf @ f64(k_cache).transpose(0, 1, 3, 2)
    s_new = qf @ f64(k_new).transpose(0, 1, 3, 2)
    s = np.concatenate([s_cache, s_new], axis=-1) * (1.0 / np.sqrt(DH))
    allowed = np.arange(P + S)[None, :] <= np.arange(S)[:, None] + P
    s = np.where(allowed[None, None], s, MASKED)
    e = np.exp(s - s.max(-1, keepdims=True))
    v_full = np.concatenate([f64(v_cache), f64(v_new)], axis=2)
    ctx = (mxq(e, 3, "e4m3") @ mxq(v_full, 2, "e4m3")) / e.sum(-1, keepdims=True)
    merged = ctx.transpose(0, 2, 1, 3).reshape(B, S, D)
    return mxq(merged, 2, "e4m3") @ mxq(f64(wo), 1, "e4m3").T

@@ -1,0 +1,301 @@
+from contextlib import ExitStack
+import math
+
+import concourse.mybir as mybir
+from concourse.masks import make_identity
+
+BF16 = mybir.dt.bfloat16
+F32 = mybir.dt.float32
+U32 = mybir.dt.uint32
+U8 = mybir.dt.uint8
+FP8X4 = mybir.dt.float8_e4m3fn_x4
+ALU = mybir.AluOpType
+ACT = mybir.ActivationFunctionType
+
+P = 128
+PACK = 4
+BATCH, HEADS, NEW, CACHED, HEAD_DIM, D_MODEL = 16, 4, 256, 256, 128, 1024
+KEYS = CACHED + NEW
+MERGED = HEADS * HEAD_DIM
+Q_TILES = NEW // P
+KEY_CHUNKS = KEYS // P
+BANK = 512
+SCALE = 1.0 / math.sqrt(HEAD_DIM)
+MASKED = -1.0e30
+
+UNITS = BATCH * HEADS
+WO_PAIRS = D_MODEL // (2 * P)
+PASSES_PER_BATCH = Q_TILES * (D_MODEL // BANK)
+PASSES = BATCH * PASSES_PER_BATCH
+STEPS = PASSES + 11
+
+FLOPS = 2 * BATCH * HEADS * NEW * KEYS * HEAD_DIM * 2 + 2 * BATCH * NEW * MERGED * D_MODEL
+
+
+def tile_mha_pa_t_kernel(tc, q, k_cache, v_cache, k_new, v_new, wo, out):
+    nc = tc.nc
+    with ExitStack() as stack:
+        consts = stack.enter_context(tc.tile_pool(name="consts", bufs=1))
+        loads = stack.enter_context(tc.tile_pool(name="loads", bufs=4))
+        work = stack.enter_context(tc.tile_pool(name="work", bufs=3))
+        psum_qk = stack.enter_context(tc.psum_pool(name="psum_qk", bufs=1))
+        psum_scores = stack.enter_context(tc.psum_pool(name="psum_scores", bufs=2))
+        psum_flip = stack.enter_context(tc.psum_pool(name="psum_flip", bufs=2))
+        psum_ctx = stack.enter_context(tc.psum_pool(name="psum_ctx", bufs=1))
+        psum_out = stack.enter_context(tc.psum_pool(name="psum_out", bufs=2))
+        stack.enter_context(tc.manual_schedule())
+
+        inputs, qk_t, score_banks, row_sum, inv_sum = {}, {}, {}, {}, {}
+        e_grouped, e_mx, v_grouped, v_mx, ctx = {}, {}, {}, {}, {}
+        merged, merged_grouped, merged_mx, wo_grouped, out_banks, out_rows = {}, {}, {}, {}, {}, {}
+
+        def load_batch(b):
+            q_sb = loads.tile([P, HEADS, Q_TILES, HEAD_DIM], BF16, name="q_sb")
+            k_sb = loads.tile([P, 2, HEADS, KEY_CHUNKS // 2, HEAD_DIM], BF16, name="k_sb")
+            v_sb = loads.tile([P, HEADS, PACK, HEAD_DIM], BF16, name="v_sb")
+            nc.sync.dma_start(out=q_sb[:], in_=q[b].rearrange("h (c p) d -> p h c d", p=P))
+            nc.sync.dma_start(out=k_sb[:, 0], in_=k_cache[b].rearrange("h (c p) d -> p h c d", p=P))
+            nc.sync.dma_start(out=k_sb[:, 1], in_=k_new[b].rearrange("h (c p) d -> p h c d", p=P))
+            nc.sync.dma_start(out=v_sb[:, :, 0:2, :], in_=v_cache[b].rearrange("h (p e) d -> p h e d", e=2))
+            nc.sync.dma_start(out=v_sb[:, :, 2:4, :], in_=v_new[b].rearrange("h (p e) d -> p h e d", e=2))
+            inputs[b] = (q_sb, k_sb, v_sb)
+
+        def flip_rows(rows, copy_out):
+            flipped = psum_flip.tile([P, 2, 2, P], F32, name="flipped")
+            for a in range(2):
+                words = rows[:, a, :].bitcast(F32)
+                for u in range(2):
+                    nc.tensor.transpose(flipped[:, a, u, :], words[:, u * P : (u + 1) * P], ident_f32[:])
+            grouped = work.tile([P, 2 * P * PACK], BF16, name="grouped", align_bytes=64)
+            copy_out(
+                out=grouped[:].bitcast(F32).rearrange("p (a r u) -> p a r u", a=2, u=2),
+                in_=flipped[:].rearrange("p a u r -> p a r u"),
+            )
+            return grouped
+
+        def new_mx_operand(name):
+            codes = work.tile([P, 2 * P], U32, name=name + "_codes", align_bytes=64)
+            scales = work.tile([P, 2 * P], U8, name=name + "_scales", align_bytes=64)
+            return codes[:], scales[:]
+
+        def quantise(grouped, operand):
+            codes, scales = operand
+            nc.vector.quantize_mx(out=codes.bitcast(FP8X4), scales=scales, in_=grouped[:])
+
+        def flip_q_and_k(u):
+            if not 0 <= u < UNITS:
+                return
+            b, h = divmod(u, HEADS)
+            q_sb, k_sb = inputs[b][0:2]
+            qk_flipped = psum_qk.tile([P, Q_TILES + KEY_CHUNKS, P], BF16, name="qk_flipped")
+            for c in range(Q_TILES):
+                nc.tensor.transpose(qk_flipped[:, c, :], q_sb[:, h, c, :], ident_bf[:])
+            for c in range(KEY_CHUNKS):
+                nc.tensor.transpose(qk_flipped[:, Q_TILES + c, :], k_sb[:, c // 2, h, c % 2, :], ident_bf[:])
+            qk_t[u] = work.tile([P, Q_TILES + KEY_CHUNKS, P], BF16, name="qk_t")
+            nc.scalar.copy(out=qk_t[u][:], in_=qk_flipped[:])
+
+        def score(u):
+            if not 0 <= u < UNITS:
+                return
+            score_banks[u] = []
+            for a in range(Q_TILES):
+                seen = CACHED + (a + 1) * P
+                scores = psum_scores.tile([P, BANK], F32, name="scores")
+                nc.tensor.matmul(
+                    out=scores[:, 0:seen],
+                    lhsT=qk_t[u][:, a, :],
+                    rhs=qk_t[u][:, Q_TILES : Q_TILES + seen // P, :].rearrange("d c k -> d (c k)"),
+                    start=True,
+                    stop=False,
+                )
+                nc.tensor.matmul(
+                    out=scores[:, seen - P : seen], lhsT=ident_bf[:], rhs=causal_bf[:], start=False, stop=True
+                )
+                score_banks[u].append(scores)
+
+        def exponentiate(u):
+            if not 0 <= u < UNITS:
+                return
+            minus_s = work.tile([P, Q_TILES, KEYS], F32, name="minus_s")
+            minus_max = work.tile([P, Q_TILES], F32, name="minus_max")
+            row_sum[u] = work.tile([P, Q_TILES], F32, name="row_sum")
+            for a in range(Q_TILES):
+                seen = CACHED + (a + 1) * P
+                nc.vector.tensor_scalar(
+                    out=minus_s[:, a, 0:seen],
+                    in0=score_banks[u][a][:, 0:seen],
+                    scalar1=-SCALE,
+                    scalar2=None,
+                    op0=ALU.mult,
+                    op1=ALU.min,
+                    accum_out=minus_max[:, a : a + 1],
+                )
+                nc.scalar.activation(
+                    out=e_tiles[u % len(e_tiles)][:, a, 0:seen],
+                    in_=minus_s[:, a, 0:seen],
+                    func=ACT.Exp,
+                    bias=minus_max[:, a : a + 1],
+                    scale=-1.0,
+                    accum_out=row_sum[u][:, a : a + 1],
+                )
+
+        def flip_e(u):
+            if 0 <= u < UNITS:
+                e_grouped[u] = flip_rows(e_tiles[u % len(e_tiles)][:], nc.vector.tensor_copy)
+
+        def regroup_v(u):
+            if not 0 <= u < UNITS:
+                return
+            b, h = divmod(u, HEADS)
+            v_sb = inputs[b][2]
+            v_grouped[u] = work.tile([P, HEAD_DIM * PACK], BF16, name="v_grouped", align_bytes=64)
+            nc.vector.tensor_copy(
+                out=v_grouped[u][:].rearrange("p (c i t) -> p c t i", i=4, t=PACK),
+                in_=v_sb[:, h, :, :].rearrange("p t (c i) -> p c t i", i=4),
+            )
+
+        def quantise_e(u):
+            if 0 <= u < UNITS:
+                e_mx[u] = new_mx_operand("e")
+                quantise(e_grouped[u], e_mx[u])
+
+        def quantise_v(u):
+            if not 0 <= u < UNITS:
+                return
+            v_codes = work.tile([P, HEAD_DIM], U32, name="v_codes", align_bytes=64)
+            v_scales = work.tile([P, HEAD_DIM], U8, name="v_scales", align_bytes=64)
+            v_mx[u] = (v_codes[:], v_scales[:])
+            quantise(v_grouped[u], v_mx[u])
+            inv_sum[u] = work.tile([P, Q_TILES], F32, name="inv_sum")
+            nc.vector.reciprocal(out=inv_sum[u][:], in_=row_sum[u][:])
+
+        def attend(u):
+            if not 0 <= u < UNITS:
+                return
+            e_codes, e_scales = e_mx[u]
+            v_codes, v_scales = v_mx[u]
+            ctx[u] = psum_ctx.tile([P, Q_TILES, HEAD_DIM], F32, name="ctx")
+            for a in range(Q_TILES):
+                rows = slice(a * P, (a + 1) * P)
+                nc.tensor.matmul_mx(
+                    out=ctx[u][:, a, :],
+                    lhsT=e_codes[:, rows].bitcast(FP8X4),
+                    lhsT_scale=e_scales[:, rows],
+                    rhs=v_codes.bitcast(FP8X4),
+                    rhs_scale=v_scales,
+                    start=True,
+                    stop=True,
+                )
+
+        def normalise(u):
+            if not 0 <= u < UNITS:
+                return
+            b, h = divmod(u, HEADS)
+            if h == 0:
+                merged[b] = work.tile([P, Q_TILES, MERGED], BF16, name="merged")
+            for a in range(Q_TILES):
+                nc.scalar.activation(
+                    out=merged[b][:, a, h * HEAD_DIM : (h + 1) * HEAD_DIM],
+                    in_=ctx[u][:, a, :],
+                    func=ACT.Copy,
+                    scale=inv_sum[u][:, a : a + 1],
+                )
+
+        def flip_wo(i):
+            if 0 <= i < WO_PAIRS:
+                wo_grouped[i] = flip_rows(wo_sb[:, 2 * i : 2 * i + 2, :], nc.scalar.copy)
+
+        def quantise_wo(i):
+            if 0 <= i < WO_PAIRS:
+                cols = slice(2 * i * P, (2 * i + 2) * P)
+                quantise(wo_grouped[i], (wo_codes[:, cols], wo_scales[:, cols]))
+
+        def flip_merged(b):
+            if 0 <= b < BATCH:
+                merged_grouped[b] = flip_rows(merged[b][:], nc.scalar.copy)
+
+        def quantise_merged(b):
+            if 0 <= b < BATCH:
+                merged_mx[b] = new_mx_operand("merged")
+                quantise(merged_grouped[b], merged_mx[b])
+
+        def project(j):
+            if not 0 <= j < PASSES:
+                return
+            m_codes, m_scales = merged_mx[j // PASSES_PER_BATCH]
+            a, n = divmod(j % PASSES_PER_BATCH, D_MODEL // BANK)
+            rows = slice(a * P, (a + 1) * P)
+            cols = slice(n * BANK, (n + 1) * BANK)
+            out_banks[j] = psum_out.tile([P, BANK], F32, name="out_ps")
+            nc.tensor.matmul_mx(
+                out=out_banks[j][:],
+                lhsT=m_codes[:, rows].bitcast(FP8X4),
+                lhsT_scale=m_scales[:, rows],
+                rhs=wo_codes[:, cols].bitcast(FP8X4),
+                rhs_scale=wo_scales[:, cols],
+                start=True,
+                stop=True,
+            )
+
+        def store_projection(j):
+            if not 0 <= j < PASSES:
+                return
+            b = j // PASSES_PER_BATCH
+            a, n = divmod(j % PASSES_PER_BATCH, D_MODEL // BANK)
+            if n == 0:
+                out_rows[(b, a)] = work.tile([P, D_MODEL], F32, name="out_sb")
+            nc.scalar.copy(out=out_rows[(b, a)][:, n * BANK : (n + 1) * BANK], in_=out_banks[j][:])
+            if n == D_MODEL // BANK - 1:
+                nc.sync.dma_start(out=out[b, a * P : (a + 1) * P, :], in_=out_rows[(b, a)][:])
+
+        load_batch(0)
+        wo_sb = consts.tile([P, D_MODEL // P, MERGED], BF16, name="wo_sb")
+        nc.sync.dma_start(out=wo_sb[:], in_=wo.rearrange("(j p) k -> p j k", p=P))
+        load_batch(1)
+
+        ident_bf = consts.tile([P, P], BF16, name="ident_bf")
+        make_identity(nc, ident_bf[:])
+        ident_f32 = consts.tile([P, P], F32, name="ident_f32")
+        make_identity(nc, ident_f32[:])
+        causal_f32 = consts.tile([P, P], F32, name="causal_f32")
+        nc.gpsimd.memset(causal_f32[:], 0.0)
+        nc.gpsimd.affine_select(
+            out=causal_f32[:],
+            in_=causal_f32[:],
+            pattern=[[-1, P]],
+            compare_op=ALU.is_ge,
+            fill=MASKED,
+            base=0,
+            channel_multiplier=1,
+        )
+        causal_bf = consts.tile([P, P], BF16, name="causal_bf")
+        nc.vector.tensor_copy(out=causal_bf[:], in_=causal_f32[:])
+        e_tiles = []
+        for i in range(3):
+            e_tile = consts.tile([P, Q_TILES, KEYS], BF16, name="e_%d" % i)
+            nc.vector.memset(e_tile[:, 0, KEYS - P : KEYS], 0.0)
+            e_tiles.append(e_tile)
+        wo_codes = consts.tile([P, D_MODEL], U32, name="wo_codes", align_bytes=64)
+        wo_scales = consts.tile([P, D_MODEL], U8, name="wo_scales", align_bytes=64)
+
+        for step in range(STEPS):
+            if step % HEADS == 0 and step // HEADS + 2 < BATCH:
+                load_batch(step // HEADS + 2)
+            attend(step - 4)
+            project(step - 10)
+            store_projection(step - 11)
+            normalise(step - 4)
+            exponentiate(step - 2)
+            flip_e(step - 3)
+            flip_q_and_k(step)
+            flip_wo(step - 4)
+            if step % HEADS == 0:
+                flip_merged(step // HEADS - 2)
+            score(step - 1)
+            regroup_v(step - 3)
+            quantise_e(step - 3)
+            quantise_v(step - 3)
+            quantise_wo(step - 5)
+            if step % HEADS == 1:
+                quantise_merged(step // HEADS - 2)

@@ -195,11 +195,10 @@ def tile_mha_pa_t_kernel(tc, q, k_cache, v_cache, k_new, v_new, wo, out):
             if h == 0:
                 merged[b] = work.tile([P, Q_TILES, MERGED], BF16, name="merged")
             for a in range(Q_TILES):
-                nc.scalar.activation(
+                nc.vector.tensor_scalar_mul(
                     out=merged[b][:, a, h * HEAD_DIM : (h + 1) * HEAD_DIM],
-                    in_=ctx[u][:, a, :],
-                    func=ACT.Copy,
-                    scale=inv_sum[u][:, a : a + 1],
+                    in0=ctx[u][:, a, :],
+                    scalar1=inv_sum[u][:, a : a + 1],
                 )
 
         def flip_wo(i):
@@ -285,8 +284,8 @@ def tile_mha_pa_t_kernel(tc, q, k_cache, v_cache, k_new, v_new, wo, out):
             attend(step - 4)
             project(step - 10)
             store_projection(step - 11)
-            normalise(step - 4)
             exponentiate(step - 2)
+            normalise(step - 4)
             flip_e(step - 3)
             flip_q_and_k(step)
             flip_wo(step - 4)

@@ -45,9 +45,10 @@ def tile_mha_pa_t_kernel(tc, q, k_cache, v_cache, k_new, v_new, wo, out):
         psum_out = stack.enter_context(tc.psum_pool(name="psum_out", bufs=2))
         stack.enter_context(tc.manual_schedule())
 
-        inputs, qk_t, score_banks, row_sum, inv_sum = {}, {}, {}, {}, {}
-        e_grouped, e_mx, v_grouped, v_mx, ctx = {}, {}, {}, {}, {}
-        merged, merged_grouped, merged_mx, wo_grouped, out_banks, out_rows = {}, {}, {}, {}, {}, {}
+        inputs, qk_flipped, qk_t, score_banks, row_sum, inv_sum = {}, {}, {}, {}, {}, {}
+        e_flipped, e_grouped, e_mx, v_grouped, v_mx, ctx = {}, {}, {}, {}, {}, {}
+        merged, merged_flipped, merged_grouped, merged_mx = {}, {}, {}, {}
+        wo_flipped, wo_grouped, out_banks, out_rows = {}, {}, {}, {}
 
         def load_batch(b):
             q_sb = loads.tile([P, HEADS, Q_TILES, HEAD_DIM], BF16, name="q_sb")
@@ -60,12 +61,15 @@ def tile_mha_pa_t_kernel(tc, q, k_cache, v_cache, k_new, v_new, wo, out):
             nc.sync.dma_start(out=v_sb[:, :, 2:4, :], in_=v_new[b].rearrange("h (p e) d -> p h e d", e=2))
             inputs[b] = (q_sb, k_sb, v_sb)
 
-        def flip_rows(rows, copy_out):
+        def flip_rows(rows):
             flipped = psum_flip.tile([P, 2, 2, P], F32, name="flipped")
             for a in range(2):
                 words = rows[:, a, :].bitcast(F32)
                 for u in range(2):
                     nc.tensor.transpose(flipped[:, a, u, :], words[:, u * P : (u + 1) * P], ident_f32[:])
+            return flipped
+
+        def fetch_flipped(flipped, copy_out):
             grouped = work.tile([P, 2 * P * PACK], BF16, name="grouped", align_bytes=64)
             copy_out(
                 out=grouped[:].bitcast(F32).rearrange("p (a r u) -> p a r u", a=2, u=2),
@@ -87,13 +91,16 @@ def tile_mha_pa_t_kernel(tc, q, k_cache, v_cache, k_new, v_new, wo, out):
                 return
             b, h = divmod(u, HEADS)
             q_sb, k_sb = inputs[b][0:2]
-            qk_flipped = psum_qk.tile([P, Q_TILES + KEY_CHUNKS, P], BF16, name="qk_flipped")
+            qk_flipped[u] = psum_qk.tile([P, Q_TILES + KEY_CHUNKS, P], BF16, name="qk_flipped")
             for c in range(Q_TILES):
-                nc.tensor.transpose(qk_flipped[:, c, :], q_sb[:, h, c, :], ident_bf[:])
+                nc.tensor.transpose(qk_flipped[u][:, c, :], q_sb[:, h, c, :], ident_bf[:])
             for c in range(KEY_CHUNKS):
-                nc.tensor.transpose(qk_flipped[:, Q_TILES + c, :], k_sb[:, c // 2, h, c % 2, :], ident_bf[:])
-            qk_t[u] = work.tile([P, Q_TILES + KEY_CHUNKS, P], BF16, name="qk_t")
-            nc.scalar.copy(out=qk_t[u][:], in_=qk_flipped[:])
+                nc.tensor.transpose(qk_flipped[u][:, Q_TILES + c, :], k_sb[:, c // 2, h, c % 2, :], ident_bf[:])
+
+        def fetch_q_and_k(u):
+            if 0 <= u < UNITS:
+                qk_t[u] = work.tile([P, Q_TILES + KEY_CHUNKS, P], BF16, name="qk_t")
+                nc.scalar.copy(out=qk_t[u][:], in_=qk_flipped[u][:])
 
         def score(u):
             if not 0 <= u < UNITS:
@@ -142,7 +149,11 @@ def tile_mha_pa_t_kernel(tc, q, k_cache, v_cache, k_new, v_new, wo, out):
 
         def flip_e(u):
             if 0 <= u < UNITS:
-                e_grouped[u] = flip_rows(e_tiles[u % len(e_tiles)][:], nc.vector.tensor_copy)
+                e_flipped[u] = flip_rows(e_tiles[u % len(e_tiles)][:])
+
+        def fetch_e(u):
+            if 0 <= u < UNITS:
+                e_grouped[u] = fetch_flipped(e_flipped[u], nc.vector.tensor_copy)
 
         def regroup_v(u):
             if not 0 <= u < UNITS:
@@ -195,15 +206,20 @@ def tile_mha_pa_t_kernel(tc, q, k_cache, v_cache, k_new, v_new, wo, out):
             if h == 0:
                 merged[b] = work.tile([P, Q_TILES, MERGED], BF16, name="merged")
             for a in range(Q_TILES):
-                nc.vector.tensor_scalar_mul(
+                nc.scalar.activation(
                     out=merged[b][:, a, h * HEAD_DIM : (h + 1) * HEAD_DIM],
-                    in0=ctx[u][:, a, :],
-                    scalar1=inv_sum[u][:, a : a + 1],
+                    in_=ctx[u][:, a, :],
+                    func=ACT.Copy,
+                    scale=inv_sum[u][:, a : a + 1],
                 )
 
         def flip_wo(i):
             if 0 <= i < WO_PAIRS:
-                wo_grouped[i] = flip_rows(wo_sb[:, 2 * i : 2 * i + 2, :], nc.scalar.copy)
+                wo_flipped[i] = flip_rows(wo_sb[:, 2 * i : 2 * i + 2, :])
+
+        def fetch_wo(i):
+            if 0 <= i < WO_PAIRS:
+                wo_grouped[i] = fetch_flipped(wo_flipped[i], nc.scalar.copy)
 
         def quantise_wo(i):
             if 0 <= i < WO_PAIRS:
@@ -212,7 +228,11 @@ def tile_mha_pa_t_kernel(tc, q, k_cache, v_cache, k_new, v_new, wo, out):
 
         def flip_merged(b):
             if 0 <= b < BATCH:
-                merged_grouped[b] = flip_rows(merged[b][:], nc.scalar.copy)
+                merged_flipped[b] = flip_rows(merged[b][:])
+
+        def fetch_merged(b):
+            if 0 <= b < BATCH:
+                merged_grouped[b] = fetch_flipped(merged_flipped[b], nc.scalar.copy)
 
         def quantise_merged(b):
             if 0 <= b < BATCH:
@@ -281,17 +301,22 @@ def tile_mha_pa_t_kernel(tc, q, k_cache, v_cache, k_new, v_new, wo, out):
         for step in range(STEPS):
             if step % HEADS == 0 and step // HEADS + 2 < BATCH:
                 load_batch(step // HEADS + 2)
+            fetch_q_and_k(step - 1)
+            fetch_wo(step - 5)
+            if step % HEADS == 1:
+                fetch_merged(step // HEADS - 2)
+            store_projection(step - 11)
+            flip_e(step - 3)
             attend(step - 4)
             project(step - 10)
-            store_projection(step - 11)
             exponentiate(step - 2)
+            fetch_e(step - 3)
             normalise(step - 4)
-            flip_e(step - 3)
+            score(step - 1)
             flip_q_and_k(step)
             flip_wo(step - 4)
             if step % HEADS == 0:
                 flip_merged(step // HEADS - 2)
-            score(step - 1)
             regroup_v(step - 3)
             quantise_e(step - 3)
             quantise_v(step - 3)

@@ -46,7 +46,7 @@ def tile_mha_pa_t_kernel(tc, q, k_cache, v_cache, k_new, v_new, wo, out):
         stack.enter_context(tc.manual_schedule())
 
         inputs, qk_flipped, qk_t, score_banks, row_sum, inv_sum = {}, {}, {}, {}, {}, {}
-        e_flipped, e_grouped, e_mx, v_grouped, v_mx, ctx = {}, {}, {}, {}, {}, {}
+        e_flipped, e_grouped, e_mx, v_mx, ctx = {}, {}, {}, {}, {}
         merged, merged_flipped, merged_grouped, merged_mx = {}, {}, {}, {}
         wo_flipped, wo_grouped, out_banks, out_rows = {}, {}, {}, {}
 
@@ -160,10 +160,13 @@ def tile_mha_pa_t_kernel(tc, q, k_cache, v_cache, k_new, v_new, wo, out):
                 return
             b, h = divmod(u, HEADS)
             v_sb = inputs[b][2]
-            v_grouped[u] = work.tile([P, HEAD_DIM * PACK], BF16, name="v_grouped", align_bytes=64)
-            nc.vector.tensor_copy(
-                out=v_grouped[u][:].rearrange("p (c i t) -> p c t i", i=4, t=PACK),
-                in_=v_sb[:, h, :, :].rearrange("p t (c i) -> p c t i", i=4),
+            nc.gpsimd.tensor_scalar(
+                out=v_grouped[:].rearrange("p (d t) -> p d t", t=PACK),
+                in0=v_sb[:, h, :, :].rearrange("p t d -> p d t"),
+                scalar1=1.0,
+                scalar2=0.0,
+                op0=ALU.mult,
+                op1=ALU.add,
             )
 
         def quantise_e(u):
@@ -177,9 +180,12 @@ def tile_mha_pa_t_kernel(tc, q, k_cache, v_cache, k_new, v_new, wo, out):
             v_codes = work.tile([P, HEAD_DIM], U32, name="v_codes", align_bytes=64)
             v_scales = work.tile([P, HEAD_DIM], U8, name="v_scales", align_bytes=64)
             v_mx[u] = (v_codes[:], v_scales[:])
-            quantise(v_grouped[u], v_mx[u])
-            inv_sum[u] = work.tile([P, Q_TILES], F32, name="inv_sum")
-            nc.vector.reciprocal(out=inv_sum[u][:], in_=row_sum[u][:])
+            quantise(v_grouped, v_mx[u])
+
+        def invert_row_sum(u):
+            if 0 <= u < UNITS:
+                inv_sum[u] = work.tile([P, Q_TILES], F32, name="inv_sum")
+                nc.vector.reciprocal(out=inv_sum[u][:], in_=row_sum[u][:])
 
         def attend(u):
             if not 0 <= u < UNITS:
@@ -205,13 +211,11 @@ def tile_mha_pa_t_kernel(tc, q, k_cache, v_cache, k_new, v_new, wo, out):
             b, h = divmod(u, HEADS)
             if h == 0:
                 merged[b] = work.tile([P, Q_TILES, MERGED], BF16, name="merged")
-            for a in range(Q_TILES):
-                nc.scalar.activation(
-                    out=merged[b][:, a, h * HEAD_DIM : (h + 1) * HEAD_DIM],
-                    in_=ctx[u][:, a, :],
-                    func=ACT.Copy,
-                    scale=inv_sum[u][:, a : a + 1],
-                )
+            cols = slice(h * HEAD_DIM, (h + 1) * HEAD_DIM)
+            nc.vector.tensor_scalar_mul(out=merged[b][:, 0, cols], in0=ctx[u][:, 0, :], scalar1=inv_sum[u][:, 0:1])
+            nc.scalar.activation(
+                out=merged[b][:, 1, cols], in_=ctx[u][:, 1, :], func=ACT.Copy, scale=inv_sum[u][:, 1:2]
+            )
 
         def flip_wo(i):
             if 0 <= i < WO_PAIRS:
@@ -295,6 +299,7 @@ def tile_mha_pa_t_kernel(tc, q, k_cache, v_cache, k_new, v_new, wo, out):
             e_tile = consts.tile([P, Q_TILES, KEYS], BF16, name="e_%d" % i)
             nc.vector.memset(e_tile[:, 0, KEYS - P : KEYS], 0.0)
             e_tiles.append(e_tile)
+        v_grouped = consts.tile([P, HEAD_DIM * PACK], BF16, name="v_grouped", align_bytes=64)
         wo_codes = consts.tile([P, D_MODEL], U32, name="wo_codes", align_bytes=64)
         wo_scales = consts.tile([P, D_MODEL], U8, name="wo_scales", align_bytes=64)
 
@@ -317,9 +322,10 @@ def tile_mha_pa_t_kernel(tc, q, k_cache, v_cache, k_new, v_new, wo, out):
             flip_wo(step - 4)
             if step % HEADS == 0:
                 flip_merged(step // HEADS - 2)
-            regroup_v(step - 3)
+            invert_row_sum(step - 3)
             quantise_e(step - 3)
             quantise_v(step - 3)
+            regroup_v(step - 2)
             quantise_wo(step - 5)
             if step % HEADS == 1:
                 quantise_merged(step // HEADS - 2)

@@ -48,15 +48,16 @@ def tile_mha_pa_t_kernel(tc, q, k_cache, v_cache, k_new, v_new, wo, out):
         inputs, qk_flipped, qk_t, score_banks, row_sum, inv_sum = {}, {}, {}, {}, {}, {}
         e_flipped, e_grouped, e_mx, v_mx, ctx = {}, {}, {}, {}, {}
         merged, merged_flipped, merged_grouped, merged_mx = {}, {}, {}, {}
-        wo_flipped, wo_grouped, out_banks, out_rows = {}, {}, {}, {}
+        wo_flipped, wo_grouped, out_banks = {}, {}, {}
 
         def load_batch(b):
             q_sb = loads.tile([P, HEADS, Q_TILES, HEAD_DIM], BF16, name="q_sb")
             k_sb = loads.tile([P, 2, HEADS, KEY_CHUNKS // 2, HEAD_DIM], BF16, name="k_sb")
             v_sb = loads.tile([P, HEADS, PACK, HEAD_DIM], BF16, name="v_sb")
-            nc.sync.dma_start(out=q_sb[:], in_=q[b].rearrange("h (c p) d -> p h c d", p=P))
-            nc.sync.dma_start(out=k_sb[:, 0], in_=k_cache[b].rearrange("h (c p) d -> p h c d", p=P))
-            nc.sync.dma_start(out=k_sb[:, 1], in_=k_new[b].rearrange("h (c p) d -> p h c d", p=P))
+            for h in range(HEADS):
+                nc.sync.dma_start(out=q_sb[:, h], in_=q[b, h].rearrange("(c p) d -> p c d", p=P))
+                nc.sync.dma_start(out=k_sb[:, 0, h], in_=k_cache[b, h].rearrange("(c p) d -> p c d", p=P))
+                nc.sync.dma_start(out=k_sb[:, 1, h], in_=k_new[b, h].rearrange("(c p) d -> p c d", p=P))
             nc.sync.dma_start(out=v_sb[:, :, 0:2, :], in_=v_cache[b].rearrange("h (p e) d -> p h e d", e=2))
             nc.sync.dma_start(out=v_sb[:, :, 2:4, :], in_=v_new[b].rearrange("h (p e) d -> p h e d", e=2))
             inputs[b] = (q_sb, k_sb, v_sb)
@@ -266,11 +267,9 @@ def tile_mha_pa_t_kernel(tc, q, k_cache, v_cache, k_new, v_new, wo, out):
                 return
             b = j // PASSES_PER_BATCH
             a, n = divmod(j % PASSES_PER_BATCH, D_MODEL // BANK)
-            if n == 0:
-                out_rows[(b, a)] = work.tile([P, D_MODEL], F32, name="out_sb")
-            nc.scalar.copy(out=out_rows[(b, a)][:, n * BANK : (n + 1) * BANK], in_=out_banks[j][:])
-            if n == D_MODEL // BANK - 1:
-                nc.sync.dma_start(out=out[b, a * P : (a + 1) * P, :], in_=out_rows[(b, a)][:])
+            out_sb = work.tile([P, BANK], F32, name="out_sb")
+            nc.scalar.copy(out=out_sb[:], in_=out_banks[j][:])
+            nc.sync.dma_start(out=out[b, a * P : (a + 1) * P, n * BANK : (n + 1) * BANK], in_=out_sb[:])
 
         load_batch(0)
         wo_sb = consts.tile([P, D_MODEL // P, MERGED], BF16, name="wo_sb")

@@ -38,6 +38,7 @@ def tile_mha_pa_t_kernel(tc, q, k_cache, v_cache, k_new, v_new, wo, out):
         consts = stack.enter_context(tc.tile_pool(name="consts", bufs=1))
         loads = stack.enter_context(tc.tile_pool(name="loads", bufs=4))
         work = stack.enter_context(tc.tile_pool(name="work", bufs=3))
+        stores = stack.enter_context(tc.tile_pool(name="stores", bufs=6))
         psum_qk = stack.enter_context(tc.psum_pool(name="psum_qk", bufs=1))
         psum_scores = stack.enter_context(tc.psum_pool(name="psum_scores", bufs=2))
         psum_flip = stack.enter_context(tc.psum_pool(name="psum_flip", bufs=2))
@@ -262,13 +263,13 @@ def tile_mha_pa_t_kernel(tc, q, k_cache, v_cache, k_new, v_new, wo, out):
                 stop=True,
             )
 
-        def store_projection(j):
+        def store_projection(j, copy_out):
             if not 0 <= j < PASSES:
                 return
             b = j // PASSES_PER_BATCH
             a, n = divmod(j % PASSES_PER_BATCH, D_MODEL // BANK)
-            out_sb = work.tile([P, BANK], F32, name="out_sb")
-            nc.scalar.copy(out=out_sb[:], in_=out_banks[j][:])
+            out_sb = stores.tile([P, BANK], F32, name="out_sb")
+            copy_out(out=out_sb[:], in_=out_banks[j][:])
             nc.sync.dma_start(out=out[b, a * P : (a + 1) * P, n * BANK : (n + 1) * BANK], in_=out_sb[:])
 
         load_batch(0)
@@ -309,7 +310,8 @@ def tile_mha_pa_t_kernel(tc, q, k_cache, v_cache, k_new, v_new, wo, out):
             fetch_wo(step - 5)
             if step % HEADS == 1:
                 fetch_merged(step // HEADS - 2)
-            store_projection(step - 11)
+            vector_free = step - 3 >= UNITS
+            store_projection(step - 11, nc.vector.tensor_copy if vector_free and step % 2 else nc.scalar.copy)
             flip_e(step - 3)
             attend(step - 4)
             project(step - 10)

@@ -27,7 +27,8 @@ UNITS = BATCH * HEADS
 WO_PAIRS = D_MODEL // (2 * P)
 PASSES_PER_BATCH = Q_TILES * (D_MODEL // BANK)
 PASSES = BATCH * PASSES_PER_BATCH
-STEPS = PASSES + 11
+LAG = 12
+STEPS = PASSES + LAG + 1
 
 FLOPS = 2 * BATCH * HEADS * NEW * KEYS * HEAD_DIM * 2 + 2 * BATCH * NEW * MERGED * D_MODEL
 
@@ -46,6 +47,7 @@ def tile_mha_pa_t_kernel(tc, q, k_cache, v_cache, k_new, v_new, wo, out):
         psum_out = stack.enter_context(tc.psum_pool(name="psum_out", bufs=2))
         stack.enter_context(tc.manual_schedule())
 
+        minus_s, minus_max = {}, {}
         inputs, qk_flipped, qk_t, score_banks, row_sum, inv_sum = {}, {}, {}, {}, {}, {}
         e_flipped, e_grouped, e_mx, v_mx, ctx = {}, {}, {}, {}, {}
         merged, merged_flipped, merged_grouped, merged_mx = {}, {}, {}, {}
@@ -123,28 +125,34 @@ def tile_mha_pa_t_kernel(tc, q, k_cache, v_cache, k_new, v_new, wo, out):
                 )
                 score_banks[u].append(scores)
 
-        def exponentiate(u):
+        def negate(u):
             if not 0 <= u < UNITS:
                 return
-            minus_s = work.tile([P, Q_TILES, KEYS], F32, name="minus_s")
-            minus_max = work.tile([P, Q_TILES], F32, name="minus_max")
-            row_sum[u] = work.tile([P, Q_TILES], F32, name="row_sum")
+            minus_s[u] = work.tile([P, Q_TILES, KEYS], F32, name="minus_s")
+            minus_max[u] = work.tile([P, Q_TILES], F32, name="minus_max")
             for a in range(Q_TILES):
                 seen = CACHED + (a + 1) * P
                 nc.vector.tensor_scalar(
-                    out=minus_s[:, a, 0:seen],
+                    out=minus_s[u][:, a, 0:seen],
                     in0=score_banks[u][a][:, 0:seen],
                     scalar1=-SCALE,
                     scalar2=None,
                     op0=ALU.mult,
                     op1=ALU.min,
-                    accum_out=minus_max[:, a : a + 1],
+                    accum_out=minus_max[u][:, a : a + 1],
                 )
+
+        def exponentiate(u):
+            if not 0 <= u < UNITS:
+                return
+            row_sum[u] = work.tile([P, Q_TILES], F32, name="row_sum")
+            for a in range(Q_TILES):
+                seen = CACHED + (a + 1) * P
                 nc.scalar.activation(
                     out=e_tiles[u % len(e_tiles)][:, a, 0:seen],
-                    in_=minus_s[:, a, 0:seen],
+                    in_=minus_s[u][:, a, 0:seen],
                     func=ACT.Exp,
-                    bias=minus_max[:, a : a + 1],
+                    bias=minus_max[u][:, a : a + 1],
                     scale=-1.0,
                     accum_out=row_sum[u][:, a : a + 1],
                 )
@@ -163,7 +171,7 @@ def tile_mha_pa_t_kernel(tc, q, k_cache, v_cache, k_new, v_new, wo, out):
             b, h = divmod(u, HEADS)
             v_sb = inputs[b][2]
             nc.gpsimd.tensor_scalar(
-                out=v_grouped[:].rearrange("p (d t) -> p d t", t=PACK),
+                out=v_grouped[:, u % 2, :].rearrange("p (d t) -> p d t", t=PACK),
                 in0=v_sb[:, h, :, :].rearrange("p t d -> p d t"),
                 scalar1=1.0,
                 scalar2=0.0,
@@ -179,10 +187,14 @@ def tile_mha_pa_t_kernel(tc, q, k_cache, v_cache, k_new, v_new, wo, out):
         def quantise_v(u):
             if not 0 <= u < UNITS:
                 return
-            v_codes = work.tile([P, HEAD_DIM], U32, name="v_codes", align_bytes=64)
-            v_scales = work.tile([P, HEAD_DIM], U8, name="v_scales", align_bytes=64)
-            v_mx[u] = (v_codes[:], v_scales[:])
-            quantise(v_grouped, v_mx[u])
+            v_codes = work.tile([P, 2 * HEAD_DIM], U32, name="v_codes", align_bytes=64)
+            v_scales = work.tile([P, 2 * HEAD_DIM], U8, name="v_scales", align_bytes=64)
+            for i in range(2):
+                cols = slice(i * HEAD_DIM, (i + 1) * HEAD_DIM)
+                v_mx[u + i] = (v_codes[:, cols], v_scales[:, cols])
+            nc.vector.quantize_mx(
+                out=v_codes[:].bitcast(FP8X4), scales=v_scales[:], in_=v_grouped[:].rearrange("p i k -> p (i k)")
+            )
 
         def invert_row_sum(u):
             if 0 <= u < UNITS:
@@ -295,11 +307,11 @@ def tile_mha_pa_t_kernel(tc, q, k_cache, v_cache, k_new, v_new, wo, out):
         causal_bf = consts.tile([P, P], BF16, name="causal_bf")
         nc.vector.tensor_copy(out=causal_bf[:], in_=causal_f32[:])
         e_tiles = []
-        for i in range(3):
+        for i in range(4):
             e_tile = consts.tile([P, Q_TILES, KEYS], BF16, name="e_%d" % i)
             nc.vector.memset(e_tile[:, 0, KEYS - P : KEYS], 0.0)
             e_tiles.append(e_tile)
-        v_grouped = consts.tile([P, HEAD_DIM * PACK], BF16, name="v_grouped", align_bytes=64)
+        v_grouped = consts.tile([P, 2, HEAD_DIM * PACK], BF16, name="v_grouped", align_bytes=64)
         wo_codes = consts.tile([P, D_MODEL], U32, name="wo_codes", align_bytes=64)
         wo_scales = consts.tile([P, D_MODEL], U8, name="wo_scales", align_bytes=64)
 
@@ -308,25 +320,28 @@ def tile_mha_pa_t_kernel(tc, q, k_cache, v_cache, k_new, v_new, wo, out):
                 load_batch(step // HEADS + 2)
             fetch_q_and_k(step - 1)
             fetch_wo(step - 5)
-            if step % HEADS == 1:
+            flip_e(step - 4)
+            attend(step - 6)
+            vector_free = step - 5 >= UNITS
+            store_projection(step - LAG - 1, nc.vector.tensor_copy if vector_free and step % 2 else nc.scalar.copy)
+            if step % HEADS == 2:
                 fetch_merged(step // HEADS - 2)
-            vector_free = step - 3 >= UNITS
-            store_projection(step - 11, nc.vector.tensor_copy if vector_free and step % 2 else nc.scalar.copy)
-            flip_e(step - 3)
-            attend(step - 4)
-            project(step - 10)
-            exponentiate(step - 2)
-            fetch_e(step - 3)
-            normalise(step - 4)
+            project(step - LAG)
+            exponentiate(step - 3)
+            negate(step - 2)
+            quantise_e(step - 5)
+            if step % HEADS == 3:
+                quantise_merged(step // HEADS - 2)
+            quantise_wo(step - 6)
+            if step % 2 == 0:
+                quantise_v(step - 4)
+                regroup_v(step - 2)
+                regroup_v(step - 1)
+            invert_row_sum(step - 5)
+            fetch_e(step - 4)
+            normalise(step - 6)
             score(step - 1)
             flip_q_and_k(step)
             flip_wo(step - 4)
-            if step % HEADS == 0:
-                flip_merged(step // HEADS - 2)
-            invert_row_sum(step - 3)
-            quantise_e(step - 3)
-            quantise_v(step - 3)
-            regroup_v(step - 2)
-            quantise_wo(step - 5)
             if step % HEADS == 1:
-                quantise_merged(step // HEADS - 2)
+                flip_merged(step // HEADS - 2)

@@ -27,7 +27,7 @@ UNITS = BATCH * HEADS
 WO_PAIRS = D_MODEL // (2 * P)
 PASSES_PER_BATCH = Q_TILES * (D_MODEL // BANK)
 PASSES = BATCH * PASSES_PER_BATCH
-LAG = 12
+LAG = 13
 STEPS = PASSES + LAG + 1
 
 FLOPS = 2 * BATCH * HEADS * NEW * KEYS * HEAD_DIM * 2 + 2 * BATCH * NEW * MERGED * D_MODEL
@@ -65,13 +65,28 @@ def tile_mha_pa_t_kernel(tc, q, k_cache, v_cache, k_new, v_new, wo, out):
             nc.sync.dma_start(out=v_sb[:, :, 2:4, :], in_=v_new[b].rearrange("h (p e) d -> p h e d", e=2))
             inputs[b] = (q_sb, k_sb, v_sb)
 
+        def transpose_later(out_ap, in_ap, ident):
+            return lambda: nc.tensor.transpose(out_ap, in_ap, ident)
+
+        def matmul_later(out_ap, lhsT, rhs, start, stop):
+            return lambda: nc.tensor.matmul(out=out_ap, lhsT=lhsT, rhs=rhs, start=start, stop=stop)
+
+        def interleave(matmuls, transposes):
+            n = max(len(matmuls), 1)
+            for i in range(n):
+                if matmuls:
+                    matmuls[i]()
+                for flip in transposes[i * len(transposes) // n : (i + 1) * len(transposes) // n]:
+                    flip()
+
         def flip_rows(rows):
             flipped = psum_flip.tile([P, 2, 2, P], F32, name="flipped")
+            calls = []
             for a in range(2):
                 words = rows[:, a, :].bitcast(F32)
                 for u in range(2):
-                    nc.tensor.transpose(flipped[:, a, u, :], words[:, u * P : (u + 1) * P], ident_f32[:])
-            return flipped
+                    calls.append(transpose_later(flipped[:, a, u, :], words[:, u * P : (u + 1) * P], ident_f32[:]))
+            return flipped, calls
 
         def fetch_flipped(flipped, copy_out):
             grouped = work.tile([P, 2 * P * PACK], BF16, name="grouped", align_bytes=64)
@@ -92,14 +107,18 @@ def tile_mha_pa_t_kernel(tc, q, k_cache, v_cache, k_new, v_new, wo, out):
 
         def flip_q_and_k(u):
             if not 0 <= u < UNITS:
-                return
+                return []
+            calls = []
             b, h = divmod(u, HEADS)
             q_sb, k_sb = inputs[b][0:2]
             qk_flipped[u] = psum_qk.tile([P, Q_TILES + KEY_CHUNKS, P], BF16, name="qk_flipped")
             for c in range(Q_TILES):
-                nc.tensor.transpose(qk_flipped[u][:, c, :], q_sb[:, h, c, :], ident_bf[:])
+                calls.append(transpose_later(qk_flipped[u][:, c, :], q_sb[:, h, c, :], ident_bf[:]))
             for c in range(KEY_CHUNKS):
-                nc.tensor.transpose(qk_flipped[u][:, Q_TILES + c, :], k_sb[:, c // 2, h, c % 2, :], ident_bf[:])
+                calls.append(
+                    transpose_later(qk_flipped[u][:, Q_TILES + c, :], k_sb[:, c // 2, h, c % 2, :], ident_bf[:])
+                )
+            return calls
 
         def fetch_q_and_k(u):
             if 0 <= u < UNITS:
@@ -108,22 +127,24 @@ def tile_mha_pa_t_kernel(tc, q, k_cache, v_cache, k_new, v_new, wo, out):
 
         def score(u):
             if not 0 <= u < UNITS:
-                return
+                return []
+            calls = []
             score_banks[u] = []
             for a in range(Q_TILES):
                 seen = CACHED + (a + 1) * P
                 scores = psum_scores.tile([P, BANK], F32, name="scores")
-                nc.tensor.matmul(
-                    out=scores[:, 0:seen],
-                    lhsT=qk_t[u][:, a, :],
-                    rhs=qk_t[u][:, Q_TILES : Q_TILES + seen // P, :].rearrange("d c k -> d (c k)"),
-                    start=True,
-                    stop=False,
+                calls.append(
+                    matmul_later(
+                        scores[:, 0:seen],
+                        qk_t[u][:, a, :],
+                        qk_t[u][:, Q_TILES : Q_TILES + seen // P, :].rearrange("d c k -> d (c k)"),
+                        True,
+                        False,
+                    )
                 )
-                nc.tensor.matmul(
-                    out=scores[:, seen - P : seen], lhsT=ident_bf[:], rhs=causal_bf[:], start=False, stop=True
-                )
+                calls.append(matmul_later(scores[:, seen - P : seen], ident_bf[:], causal_bf[:], False, True))
                 score_banks[u].append(scores)
+            return calls
 
         def negate(u):
             if not 0 <= u < UNITS:
@@ -142,24 +163,26 @@ def tile_mha_pa_t_kernel(tc, q, k_cache, v_cache, k_new, v_new, wo, out):
                     accum_out=minus_max[u][:, a : a + 1],
                 )
 
-        def exponentiate(u):
+        def exponentiate(u, a):
             if not 0 <= u < UNITS:
                 return
-            row_sum[u] = work.tile([P, Q_TILES], F32, name="row_sum")
-            for a in range(Q_TILES):
-                seen = CACHED + (a + 1) * P
-                nc.scalar.activation(
-                    out=e_tiles[u % len(e_tiles)][:, a, 0:seen],
-                    in_=minus_s[u][:, a, 0:seen],
-                    func=ACT.Exp,
-                    bias=minus_max[u][:, a : a + 1],
-                    scale=-1.0,
-                    accum_out=row_sum[u][:, a : a + 1],
-                )
+            if a == 0:
+                row_sum[u] = work.tile([P, Q_TILES], F32, name="row_sum")
+            seen = CACHED + (a + 1) * P
+            nc.scalar.activation(
+                out=e_tiles[u % len(e_tiles)][:, a, 0:seen],
+                in_=minus_s[u][:, a, 0:seen],
+                func=ACT.Exp,
+                bias=minus_max[u][:, a : a + 1],
+                scale=-1.0,
+                accum_out=row_sum[u][:, a : a + 1],
+            )
 
         def flip_e(u):
             if 0 <= u < UNITS:
-                e_flipped[u] = flip_rows(e_tiles[u % len(e_tiles)][:])
+                e_flipped[u], calls = flip_rows(e_tiles[u % len(e_tiles)][:])
+                return calls
+            return []
 
         def fetch_e(u):
             if 0 <= u < UNITS:
@@ -233,7 +256,9 @@ def tile_mha_pa_t_kernel(tc, q, k_cache, v_cache, k_new, v_new, wo, out):
 
         def flip_wo(i):
             if 0 <= i < WO_PAIRS:
-                wo_flipped[i] = flip_rows(wo_sb[:, 2 * i : 2 * i + 2, :])
+                wo_flipped[i], calls = flip_rows(wo_sb[:, 2 * i : 2 * i + 2, :])
+                return calls
+            return []
 
         def fetch_wo(i):
             if 0 <= i < WO_PAIRS:
@@ -246,7 +271,9 @@ def tile_mha_pa_t_kernel(tc, q, k_cache, v_cache, k_new, v_new, wo, out):
 
         def flip_merged(b):
             if 0 <= b < BATCH:
-                merged_flipped[b] = flip_rows(merged[b][:])
+                merged_flipped[b], calls = flip_rows(merged[b][:])
+                return calls
+            return []
 
         def fetch_merged(b):
             if 0 <= b < BATCH:
@@ -320,28 +347,27 @@ def tile_mha_pa_t_kernel(tc, q, k_cache, v_cache, k_new, v_new, wo, out):
                 load_batch(step // HEADS + 2)
             fetch_q_and_k(step - 1)
             fetch_wo(step - 5)
-            flip_e(step - 4)
             attend(step - 6)
+            project(step - LAG)
             vector_free = step - 5 >= UNITS
             store_projection(step - LAG - 1, nc.vector.tensor_copy if vector_free and step % 2 else nc.scalar.copy)
-            if step % HEADS == 2:
-                fetch_merged(step // HEADS - 2)
-            project(step - LAG)
-            exponentiate(step - 3)
-            negate(step - 2)
-            quantise_e(step - 5)
             if step % HEADS == 3:
-                quantise_merged(step // HEADS - 2)
+                fetch_merged(step // HEADS - 2)
+            negate(step - 2)
+            exponentiate(step - 3, 0)
+            normalise(step - 6)
+            exponentiate(step - 3, 1)
+            quantise_e(step - 5)
+            if step % HEADS == 0:
+                quantise_merged(step // HEADS - 3)
             quantise_wo(step - 6)
             if step % 2 == 0:
                 quantise_v(step - 4)
                 regroup_v(step - 2)
                 regroup_v(step - 1)
             invert_row_sum(step - 5)
+            flips = flip_e(step - 4) + flip_q_and_k(step) + flip_wo(step - 4)
+            if step % HEADS == 2:
+                flips = flips + flip_merged(step // HEADS - 2)
+            interleave(score(step - 1), flips)
             fetch_e(step - 4)
-            normalise(step - 6)
-            score(step - 1)
-            flip_q_and_k(step)
-            flip_wo(step - 4)
-            if step % HEADS == 1:
-                flip_merged(step // HEADS - 2)

@@ -249,10 +249,13 @@ def tile_mha_pa_t_kernel(tc, q, k_cache, v_cache, k_new, v_new, wo, out):
             if h == 0:
                 merged[b] = work.tile([P, Q_TILES, MERGED], BF16, name="merged")
             cols = slice(h * HEAD_DIM, (h + 1) * HEAD_DIM)
-            nc.vector.tensor_scalar_mul(out=merged[b][:, 0, cols], in0=ctx[u][:, 0, :], scalar1=inv_sum[u][:, 0:1])
-            nc.scalar.activation(
-                out=merged[b][:, 1, cols], in_=ctx[u][:, 1, :], func=ACT.Copy, scale=inv_sum[u][:, 1:2]
-            )
+            for a in range(Q_TILES):
+                if a == 0 and h % 2 == 0:
+                    nc.vector.tensor_scalar_mul(out=merged[b][:, a, cols], in0=ctx[u][:, a, :], scalar1=inv_sum[u][:, a : a + 1])
+                else:
+                    nc.scalar.activation(
+                        out=merged[b][:, a, cols], in_=ctx[u][:, a, :], func=ACT.Copy, scale=inv_sum[u][:, a : a + 1]
+                    )
 
         def flip_wo(i):
             if 0 <= i < WO_PAIRS:

@@ -111,7 +111,12 @@ def tile_mha_pa_t_kernel(tc, q, k_cache, v_cache, k_new, v_new, wo, out):
             calls = []
             b, h = divmod(u, HEADS)
             q_sb, k_sb = inputs[b][0:2]
-            qk_flipped[u] = psum_qk.tile([P, Q_TILES + KEY_CHUNKS, P], BF16, name="qk_flipped")
+            if u == 1:
+                qk_flipped[u] = psum_ctx.tile([P, Q_TILES + KEY_CHUNKS, P], BF16, name="ctx")
+            elif u == 2:
+                qk_flipped[u] = psum_out.tile([P, Q_TILES + KEY_CHUNKS, P], BF16, name="out_ps")
+            else:
+                qk_flipped[u] = psum_qk.tile([P, Q_TILES + KEY_CHUNKS, P], BF16, name="qk_flipped")
             for c in range(Q_TILES):
                 calls.append(transpose_later(qk_flipped[u][:, c, :], q_sb[:, h, c, :], ident_bf[:]))
             for c in range(KEY_CHUNKS):
@@ -166,8 +171,8 @@ def tile_mha_pa_t_kernel(tc, q, k_cache, v_cache, k_new, v_new, wo, out):
         def exponentiate(u, a):
             if not 0 <= u < UNITS:
                 return
-            if a == 0:
-                row_sum[u] = work.tile([P, Q_TILES], F32, name="row_sum")
+            if a == 0 and u % 2 == 0:
+                row_sum[u // 2] = work.tile([P, 2, Q_TILES], F32, name="row_sum")
             seen = CACHED + (a + 1) * P
             nc.scalar.activation(
                 out=e_tiles[u % len(e_tiles)][:, a, 0:seen],
@@ -175,7 +180,7 @@ def tile_mha_pa_t_kernel(tc, q, k_cache, v_cache, k_new, v_new, wo, out):
                 func=ACT.Exp,
                 bias=minus_max[u][:, a : a + 1],
                 scale=-1.0,
-                accum_out=row_sum[u][:, a : a + 1],
+                accum_out=row_sum[u // 2][:, u % 2, a : a + 1],
             )
 
         def flip_e(u):
@@ -194,7 +199,7 @@ def tile_mha_pa_t_kernel(tc, q, k_cache, v_cache, k_new, v_new, wo, out):
             b, h = divmod(u, HEADS)
             v_sb = inputs[b][2]
             nc.gpsimd.tensor_scalar(
-                out=v_grouped[:, u % 2, :].rearrange("p (d t) -> p d t", t=PACK),
+                out=v_grouped[:].rearrange("p (d t) -> p d t", t=PACK),
                 in0=v_sb[:, h, :, :].rearrange("p t d -> p d t"),
                 scalar1=1.0,
                 scalar2=0.0,
@@ -210,19 +215,15 @@ def tile_mha_pa_t_kernel(tc, q, k_cache, v_cache, k_new, v_new, wo, out):
         def quantise_v(u):
             if not 0 <= u < UNITS:
                 return
-            v_codes = work.tile([P, 2 * HEAD_DIM], U32, name="v_codes", align_bytes=64)
-            v_scales = work.tile([P, 2 * HEAD_DIM], U8, name="v_scales", align_bytes=64)
-            for i in range(2):
-                cols = slice(i * HEAD_DIM, (i + 1) * HEAD_DIM)
-                v_mx[u + i] = (v_codes[:, cols], v_scales[:, cols])
-            nc.vector.quantize_mx(
-                out=v_codes[:].bitcast(FP8X4), scales=v_scales[:], in_=v_grouped[:].rearrange("p i k -> p (i k)")
-            )
+            v_codes = work.tile([P, HEAD_DIM], U32, name="v_codes", align_bytes=64)
+            v_scales = work.tile([P, HEAD_DIM], U8, name="v_scales", align_bytes=64)
+            v_mx[u] = (v_codes[:], v_scales[:])
+            quantise(v_grouped, v_mx[u])
 
         def invert_row_sum(u):
             if 0 <= u < UNITS:
-                inv_sum[u] = work.tile([P, Q_TILES], F32, name="inv_sum")
-                nc.vector.reciprocal(out=inv_sum[u][:], in_=row_sum[u][:])
+                inv_sum[u // 2] = work.tile([P, 2, Q_TILES], F32, name="inv_sum")
+                nc.vector.reciprocal(out=inv_sum[u // 2][:], in_=row_sum[u // 2][:])
 
         def attend(u):
             if not 0 <= u < UNITS:
@@ -250,11 +251,11 @@ def tile_mha_pa_t_kernel(tc, q, k_cache, v_cache, k_new, v_new, wo, out):
                 merged[b] = work.tile([P, Q_TILES, MERGED], BF16, name="merged")
             cols = slice(h * HEAD_DIM, (h + 1) * HEAD_DIM)
             for a in range(Q_TILES):
-                if a == 0 and h % 2 == 0:
-                    nc.vector.tensor_scalar_mul(out=merged[b][:, a, cols], in0=ctx[u][:, a, :], scalar1=inv_sum[u][:, a : a + 1])
+                if a == 0 and h % 2 == 0 and b > 2:
+                    nc.vector.tensor_scalar_mul(out=merged[b][:, a, cols], in0=ctx[u][:, a, :], scalar1=inv_sum[u // 2][:, u % 2, a : a + 1])
                 else:
                     nc.scalar.activation(
-                        out=merged[b][:, a, cols], in_=ctx[u][:, a, :], func=ACT.Copy, scale=inv_sum[u][:, a : a + 1]
+                        out=merged[b][:, a, cols], in_=ctx[u][:, a, :], func=ACT.Copy, scale=inv_sum[u // 2][:, u % 2, a : a + 1]
                     )
 
         def flip_wo(i):
@@ -341,7 +342,7 @@ def tile_mha_pa_t_kernel(tc, q, k_cache, v_cache, k_new, v_new, wo, out):
             e_tile = consts.tile([P, Q_TILES, KEYS], BF16, name="e_%d" % i)
             nc.vector.memset(e_tile[:, 0, KEYS - P : KEYS], 0.0)
             e_tiles.append(e_tile)
-        v_grouped = consts.tile([P, 2, HEAD_DIM * PACK], BF16, name="v_grouped", align_bytes=64)
+        v_grouped = consts.tile([P, HEAD_DIM * PACK], BF16, name="v_grouped", align_bytes=64)
         wo_codes = consts.tile([P, D_MODEL], U32, name="wo_codes", align_bytes=64)
         wo_scales = consts.tile([P, D_MODEL], U8, name="wo_scales", align_bytes=64)
 
@@ -352,7 +353,7 @@ def tile_mha_pa_t_kernel(tc, q, k_cache, v_cache, k_new, v_new, wo, out):
             fetch_wo(step - 5)
             attend(step - 6)
             project(step - LAG)
-            vector_free = step - 5 >= UNITS
+            vector_free = step - 2 >= UNITS
             store_projection(step - LAG - 1, nc.vector.tensor_copy if vector_free and step % 2 else nc.scalar.copy)
             if step % HEADS == 3:
                 fetch_merged(step // HEADS - 2)
@@ -360,17 +361,22 @@ def tile_mha_pa_t_kernel(tc, q, k_cache, v_cache, k_new, v_new, wo, out):
             exponentiate(step - 3, 0)
             normalise(step - 6)
             exponentiate(step - 3, 1)
+            if step % 2 == 1:
+                invert_row_sum(step - 5)
             quantise_e(step - 5)
             if step % HEADS == 0:
                 quantise_merged(step // HEADS - 3)
             quantise_wo(step - 6)
-            if step % 2 == 0:
-                quantise_v(step - 4)
-                regroup_v(step - 2)
-                regroup_v(step - 1)
-            invert_row_sum(step - 5)
-            flips = flip_e(step - 4) + flip_q_and_k(step) + flip_wo(step - 4)
+            quantise_v(step - 5)
+            regroup_v(step - 4)
+            if step == 0:
+                for call in flip_q_and_k(0) + flip_q_and_k(1) + flip_q_and_k(2):
+                    call()
+            flips = flip_q_and_k(step) if step > 2 else []
+            flips = flips + flip_wo(step - 4)
+            first = flip_e(step - 4)
             if step % HEADS == 2:
                 flips = flips + flip_merged(step // HEADS - 2)
+            interleave([], first)
             interleave(score(step - 1), flips)
             fetch_e(step - 4)

@@ -39,7 +39,7 @@ def tile_mha_pa_t_kernel(tc, q, k_cache, v_cache, k_new, v_new, wo, out):
         consts = stack.enter_context(tc.tile_pool(name="consts", bufs=1))
         loads = stack.enter_context(tc.tile_pool(name="loads", bufs=4))
         work = stack.enter_context(tc.tile_pool(name="work", bufs=3))
-        stores = stack.enter_context(tc.tile_pool(name="stores", bufs=6))
+        stores = stack.enter_context(tc.tile_pool(name="stores", bufs=12))
         psum_qk = stack.enter_context(tc.psum_pool(name="psum_qk", bufs=1))
         psum_scores = stack.enter_context(tc.psum_pool(name="psum_scores", bufs=2))
         psum_flip = stack.enter_context(tc.psum_pool(name="psum_flip", bufs=2))
@@ -51,7 +51,7 @@ def tile_mha_pa_t_kernel(tc, q, k_cache, v_cache, k_new, v_new, wo, out):
         inputs, qk_flipped, qk_t, score_banks, row_sum, inv_sum = {}, {}, {}, {}, {}, {}
         e_flipped, e_grouped, e_mx, v_mx, ctx = {}, {}, {}, {}, {}
         merged, merged_flipped, merged_grouped, merged_mx = {}, {}, {}, {}
-        wo_flipped, wo_grouped, out_banks = {}, {}, {}
+        wo_flipped, wo_grouped, out_banks, last_flipped = {}, {}, {}, {}
 
         def load_batch(b):
             q_sb = loads.tile([P, HEADS, Q_TILES, HEAD_DIM], BF16, name="q_sb")
@@ -70,6 +70,10 @@ def tile_mha_pa_t_kernel(tc, q, k_cache, v_cache, k_new, v_new, wo, out):
 
         def matmul_later(out_ap, lhsT, rhs, start, stop):
             return lambda: nc.tensor.matmul(out=out_ap, lhsT=lhsT, rhs=rhs, start=start, stop=stop)
+
+        def flip_all(transposes):
+            for flip in transposes:
+                flip()
 
         def interleave(matmuls, transposes):
             n = max(len(matmuls), 1)
@@ -251,7 +255,7 @@ def tile_mha_pa_t_kernel(tc, q, k_cache, v_cache, k_new, v_new, wo, out):
                 merged[b] = work.tile([P, Q_TILES, MERGED], BF16, name="merged")
             cols = slice(h * HEAD_DIM, (h + 1) * HEAD_DIM)
             for a in range(Q_TILES):
-                if a == 0 and h % 2 == 0 and b > 2:
+                if a == 0 and h % 2 == 1 and b > 2:
                     nc.vector.tensor_scalar_mul(out=merged[b][:, a, cols], in0=ctx[u][:, a, :], scalar1=inv_sum[u // 2][:, u % 2, a : a + 1])
                 else:
                     nc.scalar.activation(
@@ -279,6 +283,24 @@ def tile_mha_pa_t_kernel(tc, q, k_cache, v_cache, k_new, v_new, wo, out):
                 return calls
             return []
 
+        def flip_last_merged():
+            calls = []
+            for a in range(Q_TILES):
+                last_flipped[a] = psum_flip.tile([P, 2, P], F32, name="flipped")
+                words = merged[BATCH - 1][:, a, :].bitcast(F32)
+                for i in range(2):
+                    calls.append(transpose_later(last_flipped[a][:, i, :], words[:, i * P : (i + 1) * P], ident_f32[:]))
+            return calls
+
+        def fetch_last_merged():
+            grouped = work.tile([P, 2 * P * PACK], BF16, name="grouped", align_bytes=64)
+            for a in range(Q_TILES):
+                (nc.vector.tensor_copy if a == 0 else nc.scalar.copy)(
+                    out=grouped[:].bitcast(F32).rearrange("p (a r u) -> p a r u", a=2, u=2)[:, a],
+                    in_=last_flipped[a][:].rearrange("p u r -> p r u"),
+                )
+            merged_grouped[BATCH - 1] = grouped
+
         def fetch_merged(b):
             if 0 <= b < BATCH:
                 merged_grouped[b] = fetch_flipped(merged_flipped[b], nc.scalar.copy)
@@ -295,7 +317,10 @@ def tile_mha_pa_t_kernel(tc, q, k_cache, v_cache, k_new, v_new, wo, out):
             a, n = divmod(j % PASSES_PER_BATCH, D_MODEL // BANK)
             rows = slice(a * P, (a + 1) * P)
             cols = slice(n * BANK, (n + 1) * BANK)
-            out_banks[j] = psum_out.tile([P, BANK], F32, name="out_ps")
+            if j % 2 and j + LAG > UNITS + 1:
+                out_banks[j] = psum_scores.tile([P, BANK], F32, name="scores")
+            else:
+                out_banks[j] = psum_out.tile([P, BANK], F32, name="out_ps")
             nc.tensor.matmul_mx(
                 out=out_banks[j][:],
                 lhsT=m_codes[:, rows].bitcast(FP8X4),
@@ -346,7 +371,7 @@ def tile_mha_pa_t_kernel(tc, q, k_cache, v_cache, k_new, v_new, wo, out):
         wo_codes = consts.tile([P, D_MODEL], U32, name="wo_codes", align_bytes=64)
         wo_scales = consts.tile([P, D_MODEL], U8, name="wo_scales", align_bytes=64)
 
-        for step in range(STEPS):
+        for step in range(UNITS + 3):
             if step % HEADS == 0 and step // HEADS + 2 < BATCH:
                 load_batch(step // HEADS + 2)
             fetch_q_and_k(step - 1)
@@ -354,7 +379,7 @@ def tile_mha_pa_t_kernel(tc, q, k_cache, v_cache, k_new, v_new, wo, out):
             attend(step - 6)
             project(step - LAG)
             vector_free = step - 2 >= UNITS
-            store_projection(step - LAG - 1, nc.vector.tensor_copy if vector_free and step % 2 else nc.scalar.copy)
+            store_projection(step - LAG - 1, nc.vector.tensor_copy if step == UNITS + 2 else nc.scalar.copy)
             if step % HEADS == 3:
                 fetch_merged(step // HEADS - 2)
             negate(step - 2)
@@ -380,3 +405,42 @@ def tile_mha_pa_t_kernel(tc, q, k_cache, v_cache, k_new, v_new, wo, out):
             interleave([], first)
             interleave(score(step - 1), flips)
             fetch_e(step - 4)
+
+        last_u, last_b = UNITS - 1, BATCH - 1
+        j = UNITS + 3 - LAG
+        flip_all(flip_e(last_u))
+        attend(last_u - 2)
+        project(j)
+        quantise_e(last_u - 1)
+        quantise_v(last_u - 1)
+        regroup_v(last_u)
+        store_projection(j - 1, nc.scalar.copy)
+        fetch_merged(last_b - 1)
+        invert_row_sum(last_u - 1)
+        normalise(last_u - 2)
+        fetch_e(last_u)
+        attend(last_u - 1)
+        project(j + 1)
+        quantise_merged(last_b - 1)
+        quantise_e(last_u)
+        quantise_v(last_u)
+        store_projection(j, nc.scalar.copy)
+        normalise(last_u - 1)
+        attend(last_u)
+        store_projection(j + 1, nc.scalar.copy)
+        normalise(last_u)
+        project(j + 2)
+        project(j + 3)
+        flip_all(flip_last_merged())
+        store_projection(j + 2, nc.vector.tensor_copy)
+        fetch_last_merged()
+        quantise_merged(last_b)
+        store_projection(j + 3, nc.scalar.copy)
+        project(j + 4)
+        project(j + 5)
+        store_projection(j + 4, nc.vector.tensor_copy)
+        store_projection(j + 5, nc.scalar.copy)
+        for i in range(j + 6, PASSES):
+            project(i)
+        for i in range(j + 6, PASSES):
+            store_projection(i, nc.scalar.copy if i % 2 else nc.vector.tensor_copy)

from contextlib import ExitStack
import math

import concourse.mybir as mybir
from concourse.masks import make_identity

BF16 = mybir.dt.bfloat16
F32 = mybir.dt.float32
U32 = mybir.dt.uint32
U8 = mybir.dt.uint8
FP8X4 = mybir.dt.float8_e4m3fn_x4
ALU = mybir.AluOpType
ACT = mybir.ActivationFunctionType

P = 128
PACK = 4
BATCH, HEADS, NEW, CACHED, HEAD_DIM, D_MODEL = 16, 4, 256, 256, 128, 1024
KEYS = CACHED + NEW
MERGED = HEADS * HEAD_DIM
Q_TILES = NEW // P
KEY_CHUNKS = KEYS // P
BANK = 512
SCALE = 1.0 / math.sqrt(HEAD_DIM)
MASKED = -1.0e30

UNITS = BATCH * HEADS
WO_PAIRS = D_MODEL // (2 * P)
PASSES_PER_BATCH = Q_TILES * (D_MODEL // BANK)
PASSES = BATCH * PASSES_PER_BATCH
LAG = 13
STEPS = PASSES + LAG + 1

FLOPS = 2 * BATCH * HEADS * NEW * KEYS * HEAD_DIM * 2 + 2 * BATCH * NEW * MERGED * D_MODEL


def tile_mha_pa_t_kernel(tc, q, k_cache, v_cache, k_new, v_new, wo, out):
    nc = tc.nc
    with ExitStack() as stack:
        consts = stack.enter_context(tc.tile_pool(name="consts", bufs=1))
        loads = stack.enter_context(tc.tile_pool(name="loads", bufs=4))
        work = stack.enter_context(tc.tile_pool(name="work", bufs=3))
        stores = stack.enter_context(tc.tile_pool(name="stores", bufs=12))
        psum_qk = stack.enter_context(tc.psum_pool(name="psum_qk", bufs=1))
        psum_scores = stack.enter_context(tc.psum_pool(name="psum_scores", bufs=2))
        psum_flip = stack.enter_context(tc.psum_pool(name="psum_flip", bufs=2))
        psum_ctx = stack.enter_context(tc.psum_pool(name="psum_ctx", bufs=1))
        psum_out = stack.enter_context(tc.psum_pool(name="psum_out", bufs=2))
        stack.enter_context(tc.manual_schedule())

        minus_s, minus_max = {}, {}
        inputs, qk_flipped, qk_t, score_banks, row_sum, inv_sum = {}, {}, {}, {}, {}, {}
        e_flipped, e_grouped, e_mx, v_mx, ctx = {}, {}, {}, {}, {}
        merged, merged_flipped, merged_grouped, merged_mx = {}, {}, {}, {}
        wo_flipped, wo_grouped, out_banks, last_flipped = {}, {}, {}, {}

        def load_batch(b):
            q_sb = loads.tile([P, HEADS, Q_TILES, HEAD_DIM], BF16, name="q_sb")
            k_sb = loads.tile([P, 2, HEADS, KEY_CHUNKS // 2, HEAD_DIM], BF16, name="k_sb")
            v_sb = loads.tile([P, HEADS, PACK, HEAD_DIM], BF16, name="v_sb")
            for h in range(HEADS):
                nc.sync.dma_start(out=q_sb[:, h], in_=q[b, h].rearrange("(c p) d -> p c d", p=P))
                nc.sync.dma_start(out=k_sb[:, 0, h], in_=k_cache[b, h].rearrange("(c p) d -> p c d", p=P))
                nc.sync.dma_start(out=k_sb[:, 1, h], in_=k_new[b, h].rearrange("(c p) d -> p c d", p=P))
            nc.sync.dma_start(out=v_sb[:, :, 0:2, :], in_=v_cache[b].rearrange("h (p e) d -> p h e d", e=2))
            nc.sync.dma_start(out=v_sb[:, :, 2:4, :], in_=v_new[b].rearrange("h (p e) d -> p h e d", e=2))
            inputs[b] = (q_sb, k_sb, v_sb)

        def transpose_later(out_ap, in_ap, ident):
            return lambda: nc.tensor.transpose(out_ap, in_ap, ident)

        def matmul_later(out_ap, lhsT, rhs, start, stop):
            return lambda: nc.tensor.matmul(out=out_ap, lhsT=lhsT, rhs=rhs, start=start, stop=stop)

        def flip_all(transposes):
            for flip in transposes:
                flip()

        def interleave(matmuls, transposes):
            n = max(len(matmuls), 1)
            for i in range(n):
                if matmuls:
                    matmuls[i]()
                for flip in transposes[i * len(transposes) // n : (i + 1) * len(transposes) // n]:
                    flip()

        def flip_rows(rows):
            flipped = psum_flip.tile([P, 2, 2, P], F32, name="flipped")
            calls = []
            for a in range(2):
                words = rows[:, a, :].bitcast(F32)
                for u in range(2):
                    calls.append(transpose_later(flipped[:, a, u, :], words[:, u * P : (u + 1) * P], ident_f32[:]))
            return flipped, calls

        def fetch_flipped(flipped, copy_out):
            grouped = work.tile([P, 2 * P * PACK], BF16, name="grouped", align_bytes=64)
            copy_out(
                out=grouped[:].bitcast(F32).rearrange("p (a r u) -> p a r u", a=2, u=2),
                in_=flipped[:].rearrange("p a u r -> p a r u"),
            )
            return grouped

        def new_mx_operand(name):
            codes = work.tile([P, 2 * P], U32, name=name + "_codes", align_bytes=64)
            scales = work.tile([P, 2 * P], U8, name=name + "_scales", align_bytes=64)
            return codes[:], scales[:]

        def quantise(grouped, operand):
            codes, scales = operand
            nc.vector.quantize_mx(out=codes.bitcast(FP8X4), scales=scales, in_=grouped[:])

        def flip_q_and_k(u):
            if not 0 <= u < UNITS:
                return []
            calls = []
            b, h = divmod(u, HEADS)
            q_sb, k_sb = inputs[b][0:2]
            if u == 1:
                qk_flipped[u] = psum_ctx.tile([P, Q_TILES + KEY_CHUNKS, P], BF16, name="ctx")
            elif u == 2:
                qk_flipped[u] = psum_out.tile([P, Q_TILES + KEY_CHUNKS, P], BF16, name="out_ps")
            else:
                qk_flipped[u] = psum_qk.tile([P, Q_TILES + KEY_CHUNKS, P], BF16, name="qk_flipped")
            for c in range(Q_TILES):
                calls.append(transpose_later(qk_flipped[u][:, c, :], q_sb[:, h, c, :], ident_bf[:]))
            for c in range(KEY_CHUNKS):
                calls.append(
                    transpose_later(qk_flipped[u][:, Q_TILES + c, :], k_sb[:, c // 2, h, c % 2, :], ident_bf[:])
                )
            return calls

        def fetch_q_and_k(u):
            if 0 <= u < UNITS:
                qk_t[u] = work.tile([P, Q_TILES + KEY_CHUNKS, P], BF16, name="qk_t")
                nc.scalar.copy(out=qk_t[u][:], in_=qk_flipped[u][:])

        def score(u):
            if not 0 <= u < UNITS:
                return []
            calls = []
            score_banks[u] = []
            for a in range(Q_TILES):
                seen = CACHED + (a + 1) * P
                scores = psum_scores.tile([P, BANK], F32, name="scores")
                calls.append(
                    matmul_later(
                        scores[:, 0:seen],
                        qk_t[u][:, a, :],
                        qk_t[u][:, Q_TILES : Q_TILES + seen // P, :].rearrange("d c k -> d (c k)"),
                        True,
                        False,
                    )
                )
                calls.append(matmul_later(scores[:, seen - P : seen], ident_bf[:], causal_bf[:], False, True))
                score_banks[u].append(scores)
            return calls

        def negate(u):
            if not 0 <= u < UNITS:
                return
            minus_s[u] = work.tile([P, Q_TILES, KEYS], F32, name="minus_s")
            minus_max[u] = work.tile([P, Q_TILES], F32, name="minus_max")
            for a in range(Q_TILES):
                seen = CACHED + (a + 1) * P
                nc.vector.tensor_scalar(
                    out=minus_s[u][:, a, 0:seen],
                    in0=score_banks[u][a][:, 0:seen],
                    scalar1=-SCALE,
                    scalar2=None,
                    op0=ALU.mult,
                    op1=ALU.min,
                    accum_out=minus_max[u][:, a : a + 1],
                )

        def exponentiate(u, a):
            if not 0 <= u < UNITS:
                return
            if a == 0 and u % 2 == 0:
                row_sum[u // 2] = work.tile([P, 2, Q_TILES], F32, name="row_sum")
            seen = CACHED + (a + 1) * P
            nc.scalar.activation(
                out=e_tiles[u % len(e_tiles)][:, a, 0:seen],
                in_=minus_s[u][:, a, 0:seen],
                func=ACT.Exp,
                bias=minus_max[u][:, a : a + 1],
                scale=-1.0,
                accum_out=row_sum[u // 2][:, u % 2, a : a + 1],
            )

        def flip_e(u):
            if 0 <= u < UNITS:
                e_flipped[u], calls = flip_rows(e_tiles[u % len(e_tiles)][:])
                return calls
            return []

        def fetch_e(u):
            if 0 <= u < UNITS:
                e_grouped[u] = fetch_flipped(e_flipped[u], nc.vector.tensor_copy)

        def regroup_v(u):
            if not 0 <= u < UNITS:
                return
            b, h = divmod(u, HEADS)
            v_sb = inputs[b][2]
            nc.gpsimd.tensor_scalar(
                out=v_grouped[:].rearrange("p (d t) -> p d t", t=PACK),
                in0=v_sb[:, h, :, :].rearrange("p t d -> p d t"),
                scalar1=1.0,
                scalar2=0.0,
                op0=ALU.mult,
                op1=ALU.add,
            )

        def quantise_e(u):
            if 0 <= u < UNITS:
                e_mx[u] = new_mx_operand("e")
                quantise(e_grouped[u], e_mx[u])

        def quantise_v(u):
            if not 0 <= u < UNITS:
                return
            v_codes = work.tile([P, HEAD_DIM], U32, name="v_codes", align_bytes=64)
            v_scales = work.tile([P, HEAD_DIM], U8, name="v_scales", align_bytes=64)
            v_mx[u] = (v_codes[:], v_scales[:])
            quantise(v_grouped, v_mx[u])

        def invert_row_sum(u):
            if 0 <= u < UNITS:
                inv_sum[u // 2] = work.tile([P, 2, Q_TILES], F32, name="inv_sum")
                nc.vector.reciprocal(out=inv_sum[u // 2][:], in_=row_sum[u // 2][:])

        def attend(u):
            if not 0 <= u < UNITS:
                return
            e_codes, e_scales = e_mx[u]
            v_codes, v_scales = v_mx[u]
            ctx[u] = psum_ctx.tile([P, Q_TILES, HEAD_DIM], F32, name="ctx")
            for a in range(Q_TILES):
                rows = slice(a * P, (a + 1) * P)
                nc.tensor.matmul_mx(
                    out=ctx[u][:, a, :],
                    lhsT=e_codes[:, rows].bitcast(FP8X4),
                    lhsT_scale=e_scales[:, rows],
                    rhs=v_codes.bitcast(FP8X4),
                    rhs_scale=v_scales,
                    start=True,
                    stop=True,
                )

        def normalise(u):
            if not 0 <= u < UNITS:
                return
            b, h = divmod(u, HEADS)
            if h == 0:
                merged[b] = work.tile([P, Q_TILES, MERGED], BF16, name="merged")
            cols = slice(h * HEAD_DIM, (h + 1) * HEAD_DIM)
            for a in range(Q_TILES):
                if a == 0 and h % 2 == 1 and b > 2:
                    nc.vector.tensor_scalar_mul(out=merged[b][:, a, cols], in0=ctx[u][:, a, :], scalar1=inv_sum[u // 2][:, u % 2, a : a + 1])
                else:
                    nc.scalar.activation(
                        out=merged[b][:, a, cols], in_=ctx[u][:, a, :], func=ACT.Copy, scale=inv_sum[u // 2][:, u % 2, a : a + 1]
                    )

        def flip_wo(i):
            if 0 <= i < WO_PAIRS:
                wo_flipped[i], calls = flip_rows(wo_sb[:, 2 * i : 2 * i + 2, :])
                return calls
            return []

        def fetch_wo(i):
            if 0 <= i < WO_PAIRS:
                wo_grouped[i] = fetch_flipped(wo_flipped[i], nc.scalar.copy)

        def quantise_wo(i):
            if 0 <= i < WO_PAIRS:
                cols = slice(2 * i * P, (2 * i + 2) * P)
                quantise(wo_grouped[i], (wo_codes[:, cols], wo_scales[:, cols]))

        def flip_merged(b):
            if 0 <= b < BATCH:
                merged_flipped[b], calls = flip_rows(merged[b][:])
                return calls
            return []

        def flip_last_merged():
            calls = []
            for a in range(Q_TILES):
                last_flipped[a] = psum_flip.tile([P, 2, P], F32, name="flipped")
                words = merged[BATCH - 1][:, a, :].bitcast(F32)
                for i in range(2):
                    calls.append(transpose_later(last_flipped[a][:, i, :], words[:, i * P : (i + 1) * P], ident_f32[:]))
            return calls

        def fetch_last_merged():
            grouped = work.tile([P, 2 * P * PACK], BF16, name="grouped", align_bytes=64)
            for a in range(Q_TILES):
                (nc.vector.tensor_copy if a == 0 else nc.scalar.copy)(
                    out=grouped[:].bitcast(F32).rearrange("p (a r u) -> p a r u", a=2, u=2)[:, a],
                    in_=last_flipped[a][:].rearrange("p u r -> p r u"),
                )
            merged_grouped[BATCH - 1] = grouped

        def fetch_merged(b):
            if 0 <= b < BATCH:
                merged_grouped[b] = fetch_flipped(merged_flipped[b], nc.scalar.copy)

        def quantise_merged(b):
            if 0 <= b < BATCH:
                merged_mx[b] = new_mx_operand("merged")
                quantise(merged_grouped[b], merged_mx[b])

        def project(j):
            if not 0 <= j < PASSES:
                return
            m_codes, m_scales = merged_mx[j // PASSES_PER_BATCH]
            a, n = divmod(j % PASSES_PER_BATCH, D_MODEL // BANK)
            rows = slice(a * P, (a + 1) * P)
            cols = slice(n * BANK, (n + 1) * BANK)
            if j % 2 and j + LAG > UNITS + 1:
                out_banks[j] = psum_scores.tile([P, BANK], F32, name="scores")
            else:
                out_banks[j] = psum_out.tile([P, BANK], F32, name="out_ps")
            nc.tensor.matmul_mx(
                out=out_banks[j][:],
                lhsT=m_codes[:, rows].bitcast(FP8X4),
                lhsT_scale=m_scales[:, rows],
                rhs=wo_codes[:, cols].bitcast(FP8X4),
                rhs_scale=wo_scales[:, cols],
                start=True,
                stop=True,
            )

        def store_projection(j, copy_out):
            if not 0 <= j < PASSES:
                return
            b = j // PASSES_PER_BATCH
            a, n = divmod(j % PASSES_PER_BATCH, D_MODEL // BANK)
            out_sb = stores.tile([P, BANK], F32, name="out_sb")
            copy_out(out=out_sb[:], in_=out_banks[j][:])
            nc.sync.dma_start(out=out[b, a * P : (a + 1) * P, n * BANK : (n + 1) * BANK], in_=out_sb[:])

        load_batch(0)
        wo_sb = consts.tile([P, D_MODEL // P, MERGED], BF16, name="wo_sb")
        nc.sync.dma_start(out=wo_sb[:], in_=wo.rearrange("(j p) k -> p j k", p=P))
        load_batch(1)

        ident_bf = consts.tile([P, P], BF16, name="ident_bf")
        make_identity(nc, ident_bf[:])
        ident_f32 = consts.tile([P, P], F32, name="ident_f32")
        make_identity(nc, ident_f32[:])
        causal_f32 = consts.tile([P, P], F32, name="causal_f32")
        nc.gpsimd.memset(causal_f32[:], 0.0)
        nc.gpsimd.affine_select(
            out=causal_f32[:],
            in_=causal_f32[:],
            pattern=[[-1, P]],
            compare_op=ALU.is_ge,
            fill=MASKED,
            base=0,
            channel_multiplier=1,
        )
        causal_bf = consts.tile([P, P], BF16, name="causal_bf")
        nc.vector.tensor_copy(out=causal_bf[:], in_=causal_f32[:])
        e_tiles = []
        for i in range(4):
            e_tile = consts.tile([P, Q_TILES, KEYS], BF16, name="e_%d" % i)
            nc.vector.memset(e_tile[:, 0, KEYS - P : KEYS], 0.0)
            e_tiles.append(e_tile)
        v_grouped = consts.tile([P, HEAD_DIM * PACK], BF16, name="v_grouped", align_bytes=64)
        wo_codes = consts.tile([P, D_MODEL], U32, name="wo_codes", align_bytes=64)
        wo_scales = consts.tile([P, D_MODEL], U8, name="wo_scales", align_bytes=64)

        for step in range(UNITS + 3):
            if step % HEADS == 0 and step // HEADS + 2 < BATCH:
                load_batch(step // HEADS + 2)
            fetch_q_and_k(step - 1)
            fetch_wo(step - 5)
            attend(step - 6)
            project(step - LAG)
            vector_free = step - 2 >= UNITS
            store_projection(step - LAG - 1, nc.vector.tensor_copy if step == UNITS + 2 else nc.scalar.copy)
            if step % HEADS == 3:
                fetch_merged(step // HEADS - 2)
            negate(step - 2)
            exponentiate(step - 3, 0)
            normalise(step - 6)
            exponentiate(step - 3, 1)
            if step % 2 == 1:
                invert_row_sum(step - 5)
            quantise_e(step - 5)
            if step % HEADS == 0:
                quantise_merged(step // HEADS - 3)
            quantise_wo(step - 6)
            quantise_v(step - 5)
            regroup_v(step - 4)
            if step == 0:
                for call in flip_q_and_k(0) + flip_q_and_k(1) + flip_q_and_k(2):
                    call()
            flips = flip_q_and_k(step) if step > 2 else []
            flips = flips + flip_wo(step - 4)
            first = flip_e(step - 4)
            if step % HEADS == 2:
                flips = flips + flip_merged(step // HEADS - 2)
            interleave([], first)
            interleave(score(step - 1), flips)
            fetch_e(step - 4)

        last_u, last_b = UNITS - 1, BATCH - 1
        j = UNITS + 3 - LAG
        flip_all(flip_e(last_u))
        attend(last_u - 2)
        project(j)
        quantise_e(last_u - 1)
        quantise_v(last_u - 1)
        regroup_v(last_u)
        store_projection(j - 1, nc.scalar.copy)
        fetch_merged(last_b - 1)
        invert_row_sum(last_u - 1)
        normalise(last_u - 2)
        fetch_e(last_u)
        attend(last_u - 1)
        project(j + 1)
        quantise_merged(last_b - 1)
        quantise_e(last_u)
        quantise_v(last_u)
        store_projection(j, nc.scalar.copy)
        normalise(last_u - 1)
        attend(last_u)
        store_projection(j + 1, nc.scalar.copy)
        normalise(last_u)
        project(j + 2)
        project(j + 3)
        flip_all(flip_last_merged())
        store_projection(j + 2, nc.vector.tensor_copy)
        fetch_last_merged()
        quantise_merged(last_b)
        store_projection(j + 3, nc.scalar.copy)
        project(j + 4)
        project(j + 5)
        store_projection(j + 4, nc.vector.tensor_copy)
        store_projection(j + 5, nc.scalar.copy)
        for i in range(j + 6, PASSES):
            project(i)
        for i in range(j + 6, PASSES):
            store_projection(i, nc.scalar.copy if i % 2 else nc.vector.tensor_copy)
